import numpy as np
import ml_dtypes


def mxq(x, axis, fmt="e4m3"):
    dtype, down = {"e4m3": (ml_dtypes.float8_e4m3fn, 7), "e5m2": (ml_dtypes.float8_e5m2, 14)}[fmt]
    v = np.moveaxis(np.asarray(x, np.float32).astype(ml_dtypes.bfloat16).astype(np.float64), axis, -1)
    blocks = v.reshape(v.shape[:-1] + (-1, 32))
    amax = np.abs(blocks).max(-1, keepdims=True)
    byte = np.maximum(np.where(amax > 0, np.frexp(amax)[1] - 1 + 127, 0) - down, 1)
    scale = np.exp2(byte - 127.0)
    codes = (blocks / scale).astype(np.float32).astype(dtype).astype(np.float64)
    return np.moveaxis((codes * scale).reshape(v.shape), -1, axis)


WIDE = False


def mx_kscale(k):
    if not WIDE:
        return np.ones(k)
    levels = np.array([10, -10, 5, -5, 0])
    a = np.random.permutation(np.resize(levels, k // 512 * 4)).reshape(k // 512, 4)
    idx = np.arange(k)
    return np.exp2(a[idx // 512, idx % 128 // 32])


BF16 = ml_dtypes.bfloat16


def bf(x):
    return np.asarray(x, np.float32).astype(BF16)


def f64(x):
    return np.asarray(x).astype(np.float64)


B, C, T, O, KW = 2, 512, 3072, 512, 3

EPS = 1e-8


def cosine_sim(a, b):
    na = np.maximum(np.sqrt(np.sum(a * a, axis=1)), EPS)
    nb = np.maximum(np.sqrt(np.sum(b * b, axis=1)), EPS)
    return np.sum(a * b, axis=1) / (na * nb)


def setup_inputs():
    s = mx_kscale(C)
    z = np.random.standard_normal((B, C, T + 1))
    m = np.random.standard_normal((B, 1, T))
    return {"feature": bf(np.random.standard_normal((B, C, T)) * s[None, :, None]),
            "embedding": bf(z[:, :, 1:] + m * z[:, :, :-1]),
            "weight": bf(np.random.standard_normal((O, C, KW)) / np.sqrt(C) / s[None, :, None])}


def reference(feature, embedding, weight):
    feature, embedding, weight = f64(feature), f64(embedding), f64(weight)
    emb_l = np.pad(embedding[:, :, :-1], ((0, 0), (0, 0), (1, 0)))
    emb_r = np.pad(embedding[:, :, 1:], ((0, 0), (0, 0), (0, 1)))
    sim = np.stack([cosine_sim(embedding, emb_l), cosine_sim(embedding, embedding), cosine_sim(embedding, emb_r)], axis=1)
    att = np.repeat(sim, C, axis=1)
    f_pad = np.pad(feature, ((0, 0), (0, 0), (1, 1)))
    inp_unf = np.stack([f_pad[:, :, k:k + T] for k in range(KW)], axis=2).reshape(B, C * KW, T)
    w_flat = weight.reshape(O, C * KW)
    xa = mxq(inp_unf * att, 1, "e4m3")
    return mxq(w_flat, 1, "e4m3") @ xa

@@ -1,0 +1,299 @@
+from contextlib import ExitStack
+
+import concourse.bass as bass
+import concourse.mybir as mybir
+import concourse.tile as tile
+from concourse.masks import make_identity
+
+B, C, T, O, KW = 2, 512, 3072, 512, 3
+FLOPS = 2 * B * O * C * KW * T
+
+P = 128
+F32 = mybir.dt.float32
+BF16 = mybir.dt.bfloat16
+U32 = mybir.dt.uint32
+U8 = mybir.dt.uint8
+FP8X4 = mybir.dt.float8_e4m3fn_x4
+MULT = mybir.AluOpType.mult
+ADD = mybir.AluOpType.add
+AXX = mybir.AxisListType.X
+
+NT = 512
+NBLK = T // P
+TILES = T // NT
+EP = T + 16
+FL = T + 32
+FX = 2 * FL + 16
+GN = 130
+EPS2 = 1e-16
+
+PASSES = ((0, 1, False), (1, 2, False), (2, 0, True))
+S_L, S_M1A, S_M1B, S_M2A, S_M2B, S_R = 0, 1, 2, 3, 4, 5
+
+
+def tile_attentionconv1d_t_kernel(tc, feature, embedding, weight, out):
+    nc = tc.nc
+    with ExitStack() as ctx:
+        consts = ctx.enter_context(tc.tile_pool(name="consts", bufs=1))
+        epool = ctx.enter_context(tc.tile_pool(name="epool", bufs=1))
+        fpool = ctx.enter_context(tc.tile_pool(name="fpool", bufs=2))
+        wts = ctx.enter_context(tc.tile_pool(name="wts", bufs=1))
+        cols = ctx.enter_context(tc.tile_pool(name="cols", bufs=2))
+        work = ctx.enter_context(tc.tile_pool(name="work", bufs=2))
+        spool = ctx.enter_context(tc.tile_pool(name="spool", bufs=2))
+        xpool = ctx.enter_context(tc.tile_pool(name="xpool", bufs=4))
+        qpool = ctx.enter_context(tc.tile_pool(name="qpool", bufs=6))
+        opool = ctx.enter_context(tc.tile_pool(name="opool", bufs=2))
+        ps_g = ctx.enter_context(tc.psum_pool(name="ps_g", bufs=2))
+        ps_s = ctx.enter_context(tc.psum_pool(name="ps_s", bufs=2))
+        ps_o = ctx.enter_context(tc.psum_pool(name="ps_o", bufs=3))
+        ps_m = ctx.enter_context(tc.psum_pool(name="ps_m", bufs=1))
+
+        def load_e(b):
+            e_sb = epool.tile([P, 4, EP], BF16, name="e_sb")
+            nc.gpsimd.memset(e_sb[:, :, T:EP], 0.0)
+            half = T // 2
+            for h in range(2):
+                for j in range(4):
+                    nc.sync.dma_start(
+                        out=e_sb[:, j, h * half:(h + 1) * half],
+                        in_=embedding[b, j * P:(j + 1) * P, h * half:(h + 1) * half],
+                    )
+            return e_sb
+
+        def load_f(b):
+            f_sb = fpool.tile([P, 2 * FX + 16], BF16, name="f_sb")
+            for j in range(4):
+                off = (j // 2) * FX + (j % 2) * FL
+                nc.gpsimd.memset(f_sb[:, off:off + 16], 0.0)
+                nc.gpsimd.memset(f_sb[:, off + 16 + T:off + 32 + T], 0.0)
+                nc.sync.dma_start(
+                    out=f_sb[:, off + 16:off + 16 + T],
+                    in_=feature[b, j * P:(j + 1) * P, :],
+                )
+            return f_sb
+
+        e_tiles = {}
+        f_tiles = {}
+        e_tiles[0] = load_e(0)
+        w_sb = wts.tile([P, 4, C * KW], BF16, name="w_sb")
+        nc.sync.dma_start(out=w_sb[:], in_=weight.rearrange("(ot o) c k -> o ot (c k)", o=P))
+        f_tiles[0] = load_f(0)
+
+        ident_f = consts.tile([P, P], F32, name="ident_f")
+        make_identity(nc, ident_f[:])
+        ident_b = consts.tile([P, P], BF16, name="ident_b")
+        make_identity(nc, ident_b[:])
+        band = consts.tile([P, GN], F32, name="band")
+        nc.vector.memset(band[:], 0.0)
+        nc.vector.tensor_copy(out=band[:, 0:P], in_=ident_f[:])
+        nc.vector.tensor_add(out=band[:, 1:P + 1], in0=band[:, 1:P + 1], in1=ident_f[:])
+        sh_up = consts.tile([P, P], F32, name="sh_up")
+        e_up = consts.tile([P, P], F32, name="e_up")
+        sh_dn = consts.tile([P, P], F32, name="sh_dn")
+        e_dn = consts.tile([P, P], F32, name="e_dn")
+        for t_ in (sh_up, e_up, sh_dn, e_dn):
+            nc.vector.memset(t_[:], 0.0)
+        nc.vector.tensor_copy(out=sh_up[:, 0:P - 1], in_=ident_f[:, 1:P])
+        nc.vector.tensor_copy(out=e_up[:, P - 1:P], in_=ident_f[:, 0:1])
+        nc.vector.tensor_copy(out=sh_dn[:, 1:P], in_=ident_f[:, 0:P - 1])
+        nc.vector.tensor_copy(out=e_dn[:, 0:1], in_=ident_f[:, P - 1:P])
+        par = consts.tile([P, 2], F32, name="par")
+        nc.vector.tensor_reduce(
+            out=par[:], in_=ident_f[:].rearrange("p (u v) -> p v u", v=2), axis=AXX, op=ADD
+        )
+
+        w_g = wts.tile([P, 3, 4 * NT], BF16, name="w_g", align_bytes=64)
+        w_q = wts.tile([P, 3, NT], U32, name="w_q", align_bytes=64)
+        w_s = wts.tile([P, 3, NT], U8, name="w_s", align_bytes=64)
+        for pi, (tau_a, tau_b, second) in enumerate(PASSES):
+            for ot in range(4):
+                wt = ps_o.tile([P, 1024], BF16, name="wt", tag="o")
+                for j in range(4):
+                    tau = tau_a if j < 2 else tau_b
+                    src = w_sb[:, ot, :].rearrange("o (c k) -> o c k", k=KW)[:, j * P:(j + 1) * P, tau]
+                    nc.tensor.transpose(wt[:, j * P:(j + 1) * P], src, ident_b[:])
+                nc.scalar.copy(
+                    out=w_g[:, pi, ot * NT:(ot + 1) * NT].rearrange("p (o j) -> p o j", j=4),
+                    in_=wt[:, 0:NT].rearrange("p (j o) -> p o j", j=4),
+                )
+            nc.vector.quantize_mx(
+                out=w_q[:, pi, :].bitcast(FP8X4), scales=w_s[:, pi, :], in_=w_g[:, pi, :]
+            )
+
+        def sims(b):
+            e_sb = e_tiles[b]
+            eo = cols.tile([P, NBLK, 2], F32, name="eo")
+            for g0 in range(0, NBLK, 3):
+                gp = ps_g.tile([P, 512], F32, name="gp")
+                for i in range(3):
+                    t0 = (g0 + i) * P
+                    for j in range(4):
+                        nc.tensor.matmul(
+                            out=gp[:, i * GN:(i + 1) * GN],
+                            lhsT=e_sb[:, j, t0:t0 + P],
+                            rhs=e_sb[:, j, t0:t0 + GN],
+                            start=(j == 0),
+                            stop=(j == 3),
+                        )
+                gm = work.tile([P, 3, GN], F32, name="gm")
+                nc.vector.tensor_tensor(
+                    out=gm[:],
+                    in0=gp[:, 0:3 * GN].rearrange("p (g n) -> p g n", g=3),
+                    in1=band[:].unsqueeze(1).to_broadcast([P, 3, GN]),
+                    op=MULT,
+                )
+                nc.vector.tensor_reduce(
+                    out=eo[:, g0:g0 + 3, :],
+                    in_=gm[:].rearrange("p g (u v) -> p g v u", v=2),
+                    axis=AXX,
+                    op=ADD,
+                )
+            ev = eo[:, :, 0]
+            od = eo[:, :, 1]
+            NC_ = NBLK + 2
+            cs = slice(1, NBLK + 1)
+            t_a = cols.tile([P, NBLK], F32, name="t_a")
+            t_b = cols.tile([P, NBLK], F32, name="t_b")
+            n2 = cols.tile([P, NBLK], F32, name="n2")
+            dd = cols.tile([P, NBLK], F32, name="dd")
+            nc.vector.tensor_scalar_mul(out=t_a[:], in0=ev, scalar1=par[:, 0:1])
+            nc.vector.scalar_tensor_tensor(out=n2[:], in0=od, scalar=par[:, 1:2], in1=t_a[:], op0=MULT, op1=ADD)
+            nc.vector.tensor_scalar_mul(out=t_b[:], in0=ev, scalar1=par[:, 1:2])
+            nc.vector.scalar_tensor_tensor(out=dd[:], in0=od, scalar=par[:, 0:1], in1=t_b[:], op0=MULT, op1=ADD)
+            m2 = cols.tile([P, NBLK], F32, name="m2")
+            nc.vector.tensor_scalar_max(out=m2[:], in0=n2[:], scalar1=EPS2)
+            sq = cols.tile([P, NBLK], F32, name="sq")
+            nc.scalar.sqrt(out=sq[:], in_=m2[:])
+            y0 = cols.tile([P, NBLK], F32, name="y0")
+            nc.vector.reciprocal(out=y0[:], in_=sq[:])
+            u1 = cols.tile([P, NBLK], F32, name="u1")
+            nc.vector.tensor_mul(out=u1[:], in0=y0[:], in1=y0[:])
+            u2 = cols.tile([P, NBLK], F32, name="u2")
+            nc.vector.tensor_mul(out=u2[:], in0=u1[:], in1=m2[:])
+            u3 = cols.tile([P, NBLK], F32, name="u3")
+            nc.vector.tensor_scalar(out=u3[:], in0=u2[:], scalar1=-0.5, scalar2=1.5, op0=MULT, op1=ADD)
+            rn = cols.tile([P, NC_], F32, name="rn")
+            nc.vector.memset(rn[:], 0.0)
+            nc.vector.tensor_mul(out=rn[:, cs], in0=y0[:], in1=u3[:])
+            aa = cols.tile([P, NC_], F32, name="aa")
+            nc.vector.memset(aa[:], 0.0)
+            nc.vector.tensor_mul(out=aa[:, cs], in0=dd[:], in1=rn[:, cs])
+            r2 = cols.tile([P, NBLK], F32, name="r2")
+            nc.vector.tensor_mul(out=r2[:], in0=rn[:, cs], in1=rn[:, cs])
+            sim_c = cols.tile([P, NBLK], F32, name="sim_c")
+            nc.vector.tensor_mul(out=sim_c[:], in0=n2[:], in1=r2[:])
+            sh = ps_m.tile([P, 512], F32, name="sh")
+            nc.tensor.matmul(out=sh[:, 0:NBLK], lhsT=sh_up[:], rhs=rn[:, 1:NBLK + 1], start=True, stop=False)
+            nc.tensor.matmul(out=sh[:, 0:NBLK], lhsT=e_up[:], rhs=rn[:, 2:NBLK + 2], start=False, stop=True)
+            nc.tensor.matmul(out=sh[:, 64:64 + NBLK], lhsT=sh_dn[:], rhs=aa[:, 1:NBLK + 1], start=True, stop=False)
+            nc.tensor.matmul(out=sh[:, 64:64 + NBLK], lhsT=e_dn[:], rhs=aa[:, 0:NBLK], start=False, stop=True)
+            sim_r = cols.tile([P, NBLK], F32, name="sim_r")
+            nc.vector.tensor_mul(out=sim_r[:], in0=aa[:, cs], in1=sh[:, 0:NBLK])
+            sim_l = cols.tile([P, NBLK], F32, name="sim_l")
+            nc.vector.tensor_mul(out=sim_l[:], in0=rn[:, cs], in1=sh[:, 64:64 + NBLK])
+            return sim_l, sim_c, sim_r
+
+        def prep_s(sim, tl):
+            sim_l, sim_c, sim_r = sim
+            c0 = tl * 4
+            w1 = work.tile([P, 4, 132], F32, name="w1")
+            w2 = work.tile([P, 4, 132], F32, name="w2")
+
+            def spread(dst, src, n):
+                nc.scalar.copy(out=dst, in_=src[:, c0:c0 + 4].unsqueeze(2).to_broadcast([P, 4, n]))
+
+            spread(w1[:, :, 0:43], sim_l, 43)
+            spread(w1[:, :, 43:129], sim_c, 86)
+            spread(w2[:, :, 0:86], sim_c, 86)
+            spread(w2[:, :, 86:129], sim_r, 43)
+            s_sb = spool.tile([P, 8, NT], F32, name="s_sb")
+            for slot in range(6):
+                sp = ps_s.tile([P, NT], F32, name="sp")
+                for i in range(4):
+                    if slot == S_L:
+                        src = sim_l[:, c0 + i:c0 + i + 1].to_broadcast([P, P])
+                    elif slot == S_R:
+                        src = sim_r[:, c0 + i:c0 + i + 1].to_broadcast([P, P])
+                    elif slot == S_M1A:
+                        src = w1[:, i, 0:P]
+                    elif slot == S_M1B:
+                        src = w1[:, i, 1:P + 1]
+                    elif slot == S_M2A:
+                        src = w2[:, i, 0:P]
+                    else:
+                        src = w2[:, i, 1:P + 1]
+                    nc.tensor.transpose(sp[:, i * P:(i + 1) * P], src, ident_f[:])
+                nc.scalar.copy(out=s_sb[:, slot, :], in_=sp[:])
+            return s_sb
+
+        def make_x(f_sb, s_sb, tl):
+            t0 = tl * NT
+            grouped = []
+            for tau_a, tau_b, second in PASSES:
+                delta = tau_b - tau_a
+                s0 = 16 + t0 + tau_a - 1
+                in0 = (
+                    f_sb[:, 0:2 * (FX + delta)]
+                    .rearrange("p (a x) -> p a x", a=2)[:, :, 0:2 * FL]
+                    .rearrange("p a (b l) -> p a b l", b=2)[:, :, :, s0:s0 + NT]
+                    .rearrange("p a b w -> p w a b")
+                )
+                if second:
+                    in1 = s_sb[:, 0:6, :].rearrange("p (a x) w -> p a x w", a=2)[:, :, 0:3:2, :]
+                else:
+                    in1 = s_sb[:].rearrange("p (a x) w -> p a x w", a=2)[:, :, 0:2, :]
+                xg = xpool.tile([P, NT, 4], BF16, name="xg", align_bytes=64)
+                nc.vector.tensor_tensor(
+                    out=xg[:].rearrange("p w (a b) -> p w a b", a=2),
+                    in0=in0,
+                    in1=in1.rearrange("p a b w -> p w a b"),
+                    op=MULT,
+                )
+                grouped.append(xg)
+            res = []
+            for xg in grouped:
+                xq = qpool.tile([P, NT], U32, name="xq", align_bytes=64)
+                xs = qpool.tile([P, NT], U8, name="xs", align_bytes=64)
+                nc.vector.quantize_mx(
+                    out=xq[:].bitcast(FP8X4), scales=xs[:], in_=xg[:].rearrange("p w j -> p (w j)")
+                )
+                res.append((xq, xs))
+            return res
+
+        def mm(b, tl, xqs):
+            t0 = tl * NT
+            o_sb = opool.tile([P, 4, NT], F32, name="o_sb")
+            for ot in range(4):
+                acc = ps_o.tile([P, NT], F32, name="acc", tag="o")
+                for pi in range(3):
+                    xq, xs = xqs[pi]
+                    nc.tensor.matmul_mx(
+                        out=acc[:],
+                        lhsT=w_q[:, pi, ot * P:(ot + 1) * P].bitcast(FP8X4),
+                        lhsT_scale=w_s[:, pi, ot * P:(ot + 1) * P],
+                        rhs=xq[:].bitcast(FP8X4),
+                        rhs_scale=xs[:],
+                        start=(pi == 0),
+                        stop=(pi == 2),
+                    )
+                nc.scalar.copy(out=o_sb[:, ot, :], in_=acc[:])
+            nc.sync.dma_start(
+                out=out[b].rearrange("(ot p) t -> p ot t", p=P)[:, :, t0:t0 + NT], in_=o_sb[:]
+            )
+
+        sim_t = {}
+        sim_t[0] = sims(0)
+        e_tiles[1] = load_e(1)
+        f_tiles[1] = load_f(1)
+        order = [(b, tl) for b in range(B) for tl in range(TILES)]
+        s_next = prep_s(sim_t[0], 0)
+        for idx, (b, tl) in enumerate(order):
+            s_cur = s_next
+            if idx == 1:
+                sim_t[1] = sims(1)
+            if idx + 1 < len(order):
+                nb, ntl = order[idx + 1]
+                s_next = prep_s(sim_t[nb], ntl)
+            xqs = make_x(f_tiles[b], s_cur, tl)
+            mm(b, tl, xqs)

@@ -1,8 +1,6 @@
 from contextlib import ExitStack
 
-import concourse.bass as bass
 import concourse.mybir as mybir
-import concourse.tile as tile
 from concourse.masks import make_identity
 
 B, C, T, O, KW = 2, 512, 3072, 512, 3
@@ -21,14 +19,15 @@ AXX = mybir.AxisListType.X
 NT = 512
 NBLK = T // P
 TILES = T // NT
+BPT = NT // P
 EP = T + 16
 FL = T + 32
 FX = 2 * FL + 16
 GN = 130
+GB = 3
 EPS2 = 1e-16
 
 PASSES = ((0, 1, False), (1, 2, False), (2, 0, True))
-S_L, S_M1A, S_M1B, S_M2A, S_M2B, S_R = 0, 1, 2, 3, 4, 5
 
 
 def tile_attentionconv1d_t_kernel(tc, feature, embedding, weight, out):
@@ -40,14 +39,14 @@ def tile_attentionconv1d_t_kernel(tc, feature, embedding, weight, out):
         wts = ctx.enter_context(tc.tile_pool(name="wts", bufs=1))
         cols = ctx.enter_context(tc.tile_pool(name="cols", bufs=2))
         work = ctx.enter_context(tc.tile_pool(name="work", bufs=2))
-        spool = ctx.enter_context(tc.tile_pool(name="spool", bufs=2))
-        xpool = ctx.enter_context(tc.tile_pool(name="xpool", bufs=4))
+        xpool = ctx.enter_context(tc.tile_pool(name="xpool", bufs=6))
         qpool = ctx.enter_context(tc.tile_pool(name="qpool", bufs=6))
-        opool = ctx.enter_context(tc.tile_pool(name="opool", bufs=2))
+        opool = ctx.enter_context(tc.tile_pool(name="opool", bufs=3))
         ps_g = ctx.enter_context(tc.psum_pool(name="ps_g", bufs=2))
-        ps_s = ctx.enter_context(tc.psum_pool(name="ps_s", bufs=2))
-        ps_o = ctx.enter_context(tc.psum_pool(name="ps_o", bufs=3))
-        ps_m = ctx.enter_context(tc.psum_pool(name="ps_m", bufs=1))
+        ps_x = ctx.enter_context(tc.psum_pool(name="ps_x", bufs=2))
+        ps_y = ctx.enter_context(tc.psum_pool(name="ps_y", bufs=2))
+        ps_o = ctx.enter_context(tc.psum_pool(name="ps_o", bufs=2))
+        ctx.enter_context(tc.manual_schedule())
 
         def load_e(b):
             e_sb = epool.tile([P, 4, EP], BF16, name="e_sb")
@@ -84,6 +83,9 @@ def tile_attentionconv1d_t_kernel(tc, feature, embedding, weight, out):
         make_identity(nc, ident_f[:])
         ident_b = consts.tile([P, P], BF16, name="ident_b")
         make_identity(nc, ident_b[:])
+        warm = consts.tile([P, 1], F32, name="warm")
+        nc.vector.memset(warm[:], 1.0)
+        nc.scalar.sqrt(out=warm[:], in_=warm[:])
         band = consts.tile([P, GN], F32, name="band")
         nc.vector.memset(band[:], 0.0)
         nc.vector.tensor_copy(out=band[:, 0:P], in_=ident_f[:])
@@ -106,7 +108,9 @@ def tile_attentionconv1d_t_kernel(tc, feature, embedding, weight, out):
         w_g = wts.tile([P, 3, 4 * NT], BF16, name="w_g", align_bytes=64)
         w_q = wts.tile([P, 3, NT], U32, name="w_q", align_bytes=64)
         w_s = wts.tile([P, 3, NT], U8, name="w_s", align_bytes=64)
-        for pi, (tau_a, tau_b, second) in enumerate(PASSES):
+
+        def weights_transpose(pi):
+            tau_a, tau_b, second = PASSES[pi]
             for ot in range(4):
                 wt = ps_o.tile([P, 1024], BF16, name="wt", tag="o")
                 for j in range(4):
@@ -117,54 +121,75 @@ def tile_attentionconv1d_t_kernel(tc, feature, embedding, weight, out):
                     out=w_g[:, pi, ot * NT:(ot + 1) * NT].rearrange("p (o j) -> p o j", j=4),
                     in_=wt[:, 0:NT].rearrange("p (j o) -> p o j", j=4),
                 )
+
+        def weights_quantise(pi):
             nc.vector.quantize_mx(
                 out=w_q[:, pi, :].bitcast(FP8X4), scales=w_s[:, pi, :], in_=w_g[:, pi, :]
             )
 
-        def sims(b):
+        st = {}
+
+        def gram_bank(b, k, pool, tag):
             e_sb = e_tiles[b]
-            eo = cols.tile([P, NBLK, 2], F32, name="eo")
-            for g0 in range(0, NBLK, 3):
-                gp = ps_g.tile([P, 512], F32, name="gp")
-                for i in range(3):
-                    t0 = (g0 + i) * P
-                    for j in range(4):
-                        nc.tensor.matmul(
-                            out=gp[:, i * GN:(i + 1) * GN],
-                            lhsT=e_sb[:, j, t0:t0 + P],
-                            rhs=e_sb[:, j, t0:t0 + GN],
-                            start=(j == 0),
-                            stop=(j == 3),
-                        )
-                gm = work.tile([P, 3, GN], F32, name="gm")
-                nc.vector.tensor_tensor(
-                    out=gm[:],
-                    in0=gp[:, 0:3 * GN].rearrange("p (g n) -> p g n", g=3),
-                    in1=band[:].unsqueeze(1).to_broadcast([P, 3, GN]),
-                    op=MULT,
-                )
-                nc.vector.tensor_reduce(
-                    out=eo[:, g0:g0 + 3, :],
-                    in_=gm[:].rearrange("p g (u v) -> p g v u", v=2),
-                    axis=AXX,
-                    op=ADD,
-                )
+            gp = pool.tile([P, 512], F32, name="gp", tag=tag)
+            for i in range(GB):
+                t0 = (k * GB + i) * P
+                for j in range(4):
+                    nc.tensor.matmul(
+                        out=gp[:, i * GN:(i + 1) * GN],
+                        lhsT=e_sb[:, j, t0:t0 + P],
+                        rhs=e_sb[:, j, t0:t0 + GN],
+                        start=(j == 0),
+                        stop=(j == 3),
+                    )
+            st[("gp", b, k)] = gp
+
+        def extract_bank(b, k):
+            if k == 0:
+                eo_new = cols.tile([P, NBLK, 2], F32, name="eo")
+                st[("eo", b)] = eo_new
+            eo = st[("eo", b)]
+            gp = st[("gp", b, k)]
+            gm = work.tile([P, GB, GN], F32, name="gm")
+            nc.vector.tensor_tensor(
+                out=gm[:],
+                in0=gp[:, 0:GB * GN].rearrange("p (g n) -> p g n", g=GB),
+                in1=band[:].unsqueeze(1).to_broadcast([P, GB, GN]),
+                op=MULT,
+            )
+            nc.vector.tensor_reduce(
+                out=eo[:, k * GB:(k + 1) * GB, :],
+                in_=gm[:].rearrange("p g (u v) -> p g v u", v=2),
+                axis=AXX,
+                op=ADD,
+            )
+
+        CS = slice(1, NBLK + 1)
+
+        def math_1(b):
+            eo = st[("eo", b)]
             ev = eo[:, :, 0]
             od = eo[:, :, 1]
-            NC_ = NBLK + 2
-            cs = slice(1, NBLK + 1)
             t_a = cols.tile([P, NBLK], F32, name="t_a")
             t_b = cols.tile([P, NBLK], F32, name="t_b")
             n2 = cols.tile([P, NBLK], F32, name="n2")
             dd = cols.tile([P, NBLK], F32, name="dd")
             nc.vector.tensor_scalar_mul(out=t_a[:], in0=ev, scalar1=par[:, 0:1])
-            nc.vector.scalar_tensor_tensor(out=n2[:], in0=od, scalar=par[:, 1:2], in1=t_a[:], op0=MULT, op1=ADD)
             nc.vector.tensor_scalar_mul(out=t_b[:], in0=ev, scalar1=par[:, 1:2])
+            nc.vector.scalar_tensor_tensor(out=n2[:], in0=od, scalar=par[:, 1:2], in1=t_a[:], op0=MULT, op1=ADD)
             nc.vector.scalar_tensor_tensor(out=dd[:], in0=od, scalar=par[:, 0:1], in1=t_b[:], op0=MULT, op1=ADD)
             m2 = cols.tile([P, NBLK], F32, name="m2")
             nc.vector.tensor_scalar_max(out=m2[:], in0=n2[:], scalar1=EPS2)
             sq = cols.tile([P, NBLK], F32, name="sq")
             nc.scalar.sqrt(out=sq[:], in_=m2[:])
+            rn = cols.tile([P, NBLK + 2], F32, name="rn")
+            nc.vector.memset(rn[:], 0.0)
+            aa = cols.tile([P, NBLK + 2], F32, name="aa")
+            nc.vector.memset(aa[:], 0.0)
+            st[("m1", b)] = (n2, dd, m2, sq, rn, aa)
+
+        def math_2(b):
+            n2, dd, m2, sq, rn, aa = st[("m1", b)]
             y0 = cols.tile([P, NBLK], F32, name="y0")
             nc.vector.reciprocal(out=y0[:], in_=sq[:])
             u1 = cols.tile([P, NBLK], F32, name="u1")
@@ -173,98 +198,107 @@ def tile_attentionconv1d_t_kernel(tc, feature, embedding, weight, out):
             nc.vector.tensor_mul(out=u2[:], in0=u1[:], in1=m2[:])
             u3 = cols.tile([P, NBLK], F32, name="u3")
             nc.vector.tensor_scalar(out=u3[:], in0=u2[:], scalar1=-0.5, scalar2=1.5, op0=MULT, op1=ADD)
-            rn = cols.tile([P, NC_], F32, name="rn")
-            nc.vector.memset(rn[:], 0.0)
-            nc.vector.tensor_mul(out=rn[:, cs], in0=y0[:], in1=u3[:])
-            aa = cols.tile([P, NC_], F32, name="aa")
-            nc.vector.memset(aa[:], 0.0)
-            nc.vector.tensor_mul(out=aa[:, cs], in0=dd[:], in1=rn[:, cs])
-            r2 = cols.tile([P, NBLK], F32, name="r2")
-            nc.vector.tensor_mul(out=r2[:], in0=rn[:, cs], in1=rn[:, cs])
-            sim_c = cols.tile([P, NBLK], F32, name="sim_c")
-            nc.vector.tensor_mul(out=sim_c[:], in0=n2[:], in1=r2[:])
-            sh = ps_m.tile([P, 512], F32, name="sh")
+            nc.vector.tensor_mul(out=rn[:, CS], in0=y0[:], in1=u3[:])
+            nc.vector.tensor_mul(out=aa[:, CS], in0=dd[:], in1=rn[:, CS])
+            sh = ps_g.tile([P, 512], F32, name="sh", tag="g")
             nc.tensor.matmul(out=sh[:, 0:NBLK], lhsT=sh_up[:], rhs=rn[:, 1:NBLK + 1], start=True, stop=False)
             nc.tensor.matmul(out=sh[:, 0:NBLK], lhsT=e_up[:], rhs=rn[:, 2:NBLK + 2], start=False, stop=True)
             nc.tensor.matmul(out=sh[:, 64:64 + NBLK], lhsT=sh_dn[:], rhs=aa[:, 1:NBLK + 1], start=True, stop=False)
             nc.tensor.matmul(out=sh[:, 64:64 + NBLK], lhsT=e_dn[:], rhs=aa[:, 0:NBLK], start=False, stop=True)
-            sim_r = cols.tile([P, NBLK], F32, name="sim_r")
-            nc.vector.tensor_mul(out=sim_r[:], in0=aa[:, cs], in1=sh[:, 0:NBLK])
-            sim_l = cols.tile([P, NBLK], F32, name="sim_l")
-            nc.vector.tensor_mul(out=sim_l[:], in0=rn[:, cs], in1=sh[:, 64:64 + NBLK])
-            return sim_l, sim_c, sim_r
+            r2 = cols.tile([P, NBLK], F32, name="r2")
+            nc.vector.tensor_mul(out=r2[:], in0=rn[:, CS], in1=rn[:, CS])
+            sim_c = cols.tile([P, NBLK], F32, name="sim_c")
+            nc.vector.tensor_mul(out=sim_c[:], in0=n2[:], in1=r2[:])
+            st[("m2", b)] = (sh, sim_c)
 
-        def prep_s(sim, tl):
-            sim_l, sim_c, sim_r = sim
-            c0 = tl * 4
-            w1 = work.tile([P, 4, 132], F32, name="w1")
-            w2 = work.tile([P, 4, 132], F32, name="w2")
+        def math_3(b):
+            n2, dd, m2, sq, rn, aa = st[("m1", b)]
+            sh, sim_c = st[("m2", b)]
+            sim_r = cols.tile([P, NBLK], F32, name="sim_r")
+            nc.vector.tensor_mul(out=sim_r[:], in0=aa[:, CS], in1=sh[:, 0:NBLK])
+            sim_l = cols.tile([P, NBLK], F32, name="sim_l")
+            nc.vector.tensor_mul(out=sim_l[:], in0=rn[:, CS], in1=sh[:, 64:64 + NBLK])
+            st[("sim", b)] = (sim_l, sim_c, sim_r)
+
+        def build_w(idx):
+            b, tl = idx // TILES, idx % TILES
+            sim_l, sim_c, sim_r = st[("sim", b)]
+            c0 = tl * BPT
+            w1 = work.tile([P, BPT, 132], F32, name="w1")
+            w2 = work.tile([P, BPT, 132], F32, name="w2")
 
             def spread(dst, src, n):
-                nc.scalar.copy(out=dst, in_=src[:, c0:c0 + 4].unsqueeze(2).to_broadcast([P, 4, n]))
+                nc.scalar.copy(out=dst, in_=src[:, c0:c0 + BPT].unsqueeze(2).to_broadcast([P, BPT, n]))
 
             spread(w1[:, :, 0:43], sim_l, 43)
             spread(w1[:, :, 43:129], sim_c, 86)
             spread(w2[:, :, 0:86], sim_c, 86)
             spread(w2[:, :, 86:129], sim_r, 43)
-            s_sb = spool.tile([P, 8, NT], F32, name="s_sb")
-            for slot in range(6):
-                sp = ps_s.tile([P, NT], F32, name="sp")
-                for i in range(4):
-                    if slot == S_L:
-                        src = sim_l[:, c0 + i:c0 + i + 1].to_broadcast([P, P])
-                    elif slot == S_R:
-                        src = sim_r[:, c0 + i:c0 + i + 1].to_broadcast([P, P])
-                    elif slot == S_M1A:
-                        src = w1[:, i, 0:P]
-                    elif slot == S_M1B:
-                        src = w1[:, i, 1:P + 1]
-                    elif slot == S_M2A:
-                        src = w2[:, i, 0:P]
-                    else:
-                        src = w2[:, i, 1:P + 1]
-                    nc.tensor.transpose(sp[:, i * P:(i + 1) * P], src, ident_f[:])
-                nc.scalar.copy(out=s_sb[:, slot, :], in_=sp[:])
-            return s_sb
+            st[("w", idx)] = (w1, w2)
 
-        def make_x(f_sb, s_sb, tl):
-            t0 = tl * NT
-            grouped = []
-            for tau_a, tau_b, second in PASSES:
+        def tr_block(g):
+            idx, i = g // BPT, g % BPT
+            b, tl = idx // TILES, idx % TILES
+            sim_l, sim_c, sim_r = st[("sim", b)]
+            w1, w2 = st[("w", idx)]
+            c = tl * BPT + i
+            left = sim_l[:, c:c + 1].to_broadcast([P, P])
+            right = sim_r[:, c:c + 1].to_broadcast([P, P])
+            xb = ps_x.tile([P, 512], F32, name="xb", tag="xb")
+            yb = ps_y.tile([P, 512], F32, name="yb", tag="yb")
+            for j, src in enumerate((left, w1[:, i, 0:P], w2[:, i, 1:P + 1], right)):
+                nc.tensor.transpose(xb[:, j * P:(j + 1) * P], src, ident_f[:])
+            for j, src in enumerate((left, w1[:, i, 1:P + 1], w2[:, i, 0:P], right)):
+                nc.tensor.transpose(yb[:, j * P:(j + 1) * P], src, ident_f[:])
+            st[("s", g)] = (xb, yb)
+
+        def mult_block(g):
+            idx, i = g // BPT, g % BPT
+            b, tl = idx // TILES, idx % TILES
+            f_sb = f_tiles[b]
+            if i == 0:
+                xg_new = []
+                for pi in range(3):
+                    xg = xpool.tile([P, NT, 4], BF16, name="xg", align_bytes=64)
+                    xg_new.append(xg)
+                st[("xg", idx)] = xg_new
+            xgs = st[("xg", idx)]
+            xb, yb = st[("s", g)]
+            for pi, (tau_a, tau_b, second) in enumerate(PASSES):
                 delta = tau_b - tau_a
-                s0 = 16 + t0 + tau_a - 1
+                s0 = 16 + tl * NT + i * P + tau_a - 1
                 in0 = (
                     f_sb[:, 0:2 * (FX + delta)]
                     .rearrange("p (a x) -> p a x", a=2)[:, :, 0:2 * FL]
-                    .rearrange("p a (b l) -> p a b l", b=2)[:, :, :, s0:s0 + NT]
+                    .rearrange("p a (b l) -> p a b l", b=2)[:, :, :, s0:s0 + P]
                     .rearrange("p a b w -> p w a b")
                 )
-                if second:
-                    in1 = s_sb[:, 0:6, :].rearrange("p (a x) w -> p a x w", a=2)[:, :, 0:3:2, :]
-                else:
-                    in1 = s_sb[:].rearrange("p (a x) w -> p a x w", a=2)[:, :, 0:2, :]
-                xg = xpool.tile([P, NT, 4], BF16, name="xg", align_bytes=64)
+                bank = yb if second else xb
                 nc.vector.tensor_tensor(
-                    out=xg[:].rearrange("p w (a b) -> p w a b", a=2),
+                    out=xgs[pi][:, i * P:(i + 1) * P, :].rearrange("p w (a b) -> p w a b", a=2),
                     in0=in0,
-                    in1=in1.rearrange("p a b w -> p w a b"),
+                    in1=bank[:].rearrange("p (a b w) -> p w a b", a=2, b=2),
                     op=MULT,
                 )
-                grouped.append(xg)
+
+        def quantise(idx):
             res = []
-            for xg in grouped:
+            for xg in st[("xg", idx)]:
                 xq = qpool.tile([P, NT], U32, name="xq", align_bytes=64)
                 xs = qpool.tile([P, NT], U8, name="xs", align_bytes=64)
                 nc.vector.quantize_mx(
                     out=xq[:].bitcast(FP8X4), scales=xs[:], in_=xg[:].rearrange("p w j -> p (w j)")
                 )
                 res.append((xq, xs))
-            return res
+            st[("xq", idx)] = res
 
-        def mm(b, tl, xqs):
+        def mm_half(idx, h):
+            b, tl = idx // TILES, idx % TILES
             t0 = tl * NT
-            o_sb = opool.tile([P, 4, NT], F32, name="o_sb")
-            for ot in range(4):
+            xqs = st[("xq", idx)]
+            o_sb = opool.tile([P, 2, NT], F32, name="o_sb")
+            for oo in range(2):
+                ot = 2 * h + oo
                 acc = ps_o.tile([P, NT], F32, name="acc", tag="o")
                 for pi in range(3):
                     xq, xs = xqs[pi]
@@ -277,23 +311,52 @@ def tile_attentionconv1d_t_kernel(tc, feature, embedding, weight, out):
                         start=(pi == 0),
                         stop=(pi == 2),
                     )
-                nc.scalar.copy(out=o_sb[:, ot, :], in_=acc[:])
+                nc.scalar.copy(out=o_sb[:, oo, :], in_=acc[:])
             nc.sync.dma_start(
-                out=out[b].rearrange("(ot p) t -> p ot t", p=P)[:, :, t0:t0 + NT], in_=o_sb[:]
+                out=out[b, 2 * h * P:(2 * h + 2) * P, t0:t0 + NT].rearrange("(ot p) t -> p ot t", p=P),
+                in_=o_sb[:],
             )
 
-        sim_t = {}
-        sim_t[0] = sims(0)
+        rot = ((ps_g, "g"), (ps_g, "g"), (ps_x, "xb"), (ps_x, "xb"), (ps_y, "yb"), (ps_y, "yb"), (ps_o, "o"), (ps_o, "o"))
+        NBANK = NBLK // GB
+        for k in range(NBANK):
+            gram_bank(0, k, rot[k][0], rot[k][1])
+        for k in range(NBANK):
+            extract_bank(0, k)
+        math_1(0)
+        math_2(0)
+        math_3(0)
         e_tiles[1] = load_e(1)
         f_tiles[1] = load_f(1)
-        order = [(b, tl) for b in range(B) for tl in range(TILES)]
-        s_next = prep_s(sim_t[0], 0)
-        for idx, (b, tl) in enumerate(order):
-            s_cur = s_next
-            if idx == 1:
-                sim_t[1] = sims(1)
-            if idx + 1 < len(order):
-                nb, ntl = order[idx + 1]
-                s_next = prep_s(sim_t[nb], ntl)
-            xqs = make_x(f_tiles[b], s_cur, tl)
-            mm(b, tl, xqs)
+        build_w(0)
+        tr_block(0)
+        tr_block(1)
+
+        NG = B * NBLK
+        for g in range(NG):
+            idx, i = g // BPT, g % BPT
+            if i == 0 and idx + 1 < B * TILES:
+                build_w(idx + 1)
+            mult_block(g)
+            if g + 2 < NG:
+                tr_block(g + 2)
+            if g < 3:
+                weights_transpose(g)
+            if 1 <= g < 4:
+                weights_quantise(g - 1)
+            if 4 <= g < 4 + NBANK:
+                gram_bank(1, g - 4, ps_g, "g")
+            if 5 <= g < 5 + NBANK:
+                extract_bank(1, g - 5)
+            if g == 13:
+                math_1(1)
+            if g == 14:
+                math_2(1)
+            if g == 15:
+                math_3(1)
+            if i == BPT - 1:
+                quantise(idx)
+                mm_half(idx, 0)
+            if i == 0 and idx > 0:
+                mm_half(idx - 1, 1)
+        mm_half(B * TILES - 1, 1)

@@ -27,7 +27,11 @@ GN = 130
 GB = 3
 EPS2 = 1e-16
 
-PASSES = ((0, 1, False), (1, 2, False), (2, 0, True))
+PASSES = (
+    (2, 15, ((0, 0), (1, 0), (2, 1), (3, 1)), False),
+    (2, 16, ((0, 1), (1, 1), (2, 2), (3, 2)), False),
+    (0, 17, ((2, 0), (3, 0), (0, 2), (1, 2)), True),
+)
 
 
 def tile_attentionconv1d_t_kernel(tc, feature, embedding, weight, out):
@@ -61,23 +65,33 @@ def tile_attentionconv1d_t_kernel(tc, feature, embedding, weight, out):
             return e_sb
 
         def load_f(b):
-            f_sb = fpool.tile([P, 2 * FX + 16], BF16, name="f_sb")
-            for j in range(4):
-                off = (j // 2) * FX + (j % 2) * FL
-                nc.gpsimd.memset(f_sb[:, off:off + 16], 0.0)
-                nc.gpsimd.memset(f_sb[:, off + 16 + T:off + 32 + T], 0.0)
-                nc.sync.dma_start(
-                    out=f_sb[:, off + 16:off + 16 + T],
-                    in_=feature[b, j * P:(j + 1) * P, :],
-                )
+            f_sb = fpool.tile([P, 6, FL], BF16, name="f_sb")
+            nc.gpsimd.memset(f_sb[:, :, 0:32], 0.0)
+            nc.gpsimd.memset(f_sb[:, :, T:FL], 0.0)
             return f_sb
+
+        FH = 16 + T // 2
+
+        def load_f_half(f_sb, b, h):
+            for row, ch, shift in ((2, 0, 16), (3, 1, 16), (4, 2, 15), (5, 3, 15), (0, 2, 18), (1, 3, 18)):
+                lo = max(shift, 16) if h == 0 else FH
+                hi = FH if h == 0 else shift + T
+                nc.sync.dma_start(
+                    out=f_sb[:, row, lo:hi], in_=feature[b, ch * P:(ch + 1) * P, lo - shift:hi - shift]
+                )
+
+        def fix_f(b):
+            f_sb = f_tiles[b]
+            nc.vector.tensor_copy(out=f_sb[:, 4:6, 15:16], in_=f_sb[:, 0:2, 18:19])
 
         e_tiles = {}
         f_tiles = {}
         e_tiles[0] = load_e(0)
+        f_tiles[0] = load_f(0)
+        load_f_half(f_tiles[0], 0, 0)
         w_sb = wts.tile([P, 4, C * KW], BF16, name="w_sb")
         nc.sync.dma_start(out=w_sb[:], in_=weight.rearrange("(ot o) c k -> o ot (c k)", o=P))
-        f_tiles[0] = load_f(0)
+        load_f_half(f_tiles[0], 0, 1)
 
         ident_f = consts.tile([P, P], F32, name="ident_f")
         make_identity(nc, ident_f[:])
@@ -110,12 +124,12 @@ def tile_attentionconv1d_t_kernel(tc, feature, embedding, weight, out):
         w_s = wts.tile([P, 3, NT], U8, name="w_s", align_bytes=64)
 
         def weights_transpose(pi):
-            tau_a, tau_b, second = PASSES[pi]
+            slots = PASSES[pi][2]
             for ot in range(4):
                 wt = ps_o.tile([P, 1024], BF16, name="wt", tag="o")
                 for j in range(4):
-                    tau = tau_a if j < 2 else tau_b
-                    src = w_sb[:, ot, :].rearrange("o (c k) -> o c k", k=KW)[:, j * P:(j + 1) * P, tau]
+                    ch, tau = slots[j]
+                    src = w_sb[:, ot, :].rearrange("o (c k) -> o c k", k=KW)[:, ch * P:(ch + 1) * P, tau]
                     nc.tensor.transpose(wt[:, j * P:(j + 1) * P], src, ident_b[:])
                 nc.scalar.copy(
                     out=w_g[:, pi, ot * NT:(ot + 1) * NT].rearrange("p (o j) -> p o j", j=4),
@@ -248,7 +262,7 @@ def tile_attentionconv1d_t_kernel(tc, feature, embedding, weight, out):
             yb = ps_y.tile([P, 512], F32, name="yb", tag="yb")
             for j, src in enumerate((left, w1[:, i, 0:P], w2[:, i, 1:P + 1], right)):
                 nc.tensor.transpose(xb[:, j * P:(j + 1) * P], src, ident_f[:])
-            for j, src in enumerate((left, w1[:, i, 1:P + 1], w2[:, i, 0:P], right)):
+            for j, src in enumerate((w2[:, i, 0:P], right, left, w1[:, i, 1:P + 1])):
                 nc.tensor.transpose(yb[:, j * P:(j + 1) * P], src, ident_f[:])
             st[("s", g)] = (xb, yb)
 
@@ -264,20 +278,13 @@ def tile_attentionconv1d_t_kernel(tc, feature, embedding, weight, out):
                 st[("xg", idx)] = xg_new
             xgs = st[("xg", idx)]
             xb, yb = st[("s", g)]
-            for pi, (tau_a, tau_b, second) in enumerate(PASSES):
-                delta = tau_b - tau_a
-                s0 = 16 + tl * NT + i * P + tau_a - 1
-                in0 = (
-                    f_sb[:, 0:2 * (FX + delta)]
-                    .rearrange("p (a x) -> p a x", a=2)[:, :, 0:2 * FL]
-                    .rearrange("p a (b l) -> p a b l", b=2)[:, :, :, s0:s0 + P]
-                    .rearrange("p a b w -> p w a b")
-                )
+            for pi, (r0, col0, slots, second) in enumerate(PASSES):
+                s0 = col0 + tl * NT + i * P
                 bank = yb if second else xb
                 nc.vector.tensor_tensor(
-                    out=xgs[pi][:, i * P:(i + 1) * P, :].rearrange("p w (a b) -> p w a b", a=2),
-                    in0=in0,
-                    in1=bank[:].rearrange("p (a b w) -> p w a b", a=2, b=2),
+                    out=xgs[pi][:, i * P:(i + 1) * P, :].rearrange("p (c i) j -> p c j i", i=4),
+                    in0=f_sb[:, r0:r0 + 4, s0:s0 + P].rearrange("p j (c i) -> p c j i", i=4),
+                    in1=bank[:].rearrange("p (j c i) -> p c j i", j=4, i=4),
                     op=MULT,
                 )
 
@@ -328,6 +335,9 @@ def tile_attentionconv1d_t_kernel(tc, feature, embedding, weight, out):
         math_3(0)
         e_tiles[1] = load_e(1)
         f_tiles[1] = load_f(1)
+        load_f_half(f_tiles[1], 1, 0)
+        load_f_half(f_tiles[1], 1, 1)
+        fix_f(0)
         build_w(0)
         tr_block(0)
         tr_block(1)
@@ -354,6 +364,7 @@ def tile_attentionconv1d_t_kernel(tc, feature, embedding, weight, out):
                 math_2(1)
             if g == 15:
                 math_3(1)
+                fix_f(1)
             if i == BPT - 1:
                 quantise(idx)
                 mm_half(idx, 0)

@@ -46,6 +46,7 @@ def tile_attentionconv1d_t_kernel(tc, feature, embedding, weight, out):
         xpool = ctx.enter_context(tc.tile_pool(name="xpool", bufs=6))
         qpool = ctx.enter_context(tc.tile_pool(name="qpool", bufs=6))
         opool = ctx.enter_context(tc.tile_pool(name="opool", bufs=3))
+        ypool = ctx.enter_context(tc.tile_pool(name="ypool", bufs=4))
         ps_g = ctx.enter_context(tc.psum_pool(name="ps_g", bufs=2))
         ps_x = ctx.enter_context(tc.psum_pool(name="ps_x", bufs=2))
         ps_y = ctx.enter_context(tc.psum_pool(name="ps_y", bufs=2))
@@ -264,7 +265,9 @@ def tile_attentionconv1d_t_kernel(tc, feature, embedding, weight, out):
                 nc.tensor.transpose(xb[:, j * P:(j + 1) * P], src, ident_f[:])
             for j, src in enumerate((w2[:, i, 0:P], right, left, w1[:, i, 1:P + 1])):
                 nc.tensor.transpose(yb[:, j * P:(j + 1) * P], src, ident_f[:])
-            st[("s", g)] = (xb, yb)
+            y_sb = ypool.tile([P, 512], F32, name="y_sb")
+            nc.scalar.copy(out=y_sb[:], in_=yb[:])
+            st[("s", g)] = (xb, y_sb)
 
         def mult_block(g):
             idx, i = g // BPT, g % BPT
@@ -281,23 +284,25 @@ def tile_attentionconv1d_t_kernel(tc, feature, embedding, weight, out):
             for pi, (r0, col0, slots, second) in enumerate(PASSES):
                 s0 = col0 + tl * NT + i * P
                 bank = yb if second else xb
-                nc.vector.tensor_tensor(
+                eng = nc.gpsimd if second else nc.vector
+                eng.tensor_tensor(
                     out=xgs[pi][:, i * P:(i + 1) * P, :].rearrange("p (c i) j -> p c j i", i=4),
                     in0=f_sb[:, r0:r0 + 4, s0:s0 + P].rearrange("p j (c i) -> p c j i", i=4),
                     in1=bank[:].rearrange("p (j c i) -> p c j i", j=4, i=4),
                     op=MULT,
                 )
 
-        def quantise(idx):
-            res = []
-            for xg in st[("xg", idx)]:
+        def quantise(idx, which):
+            if ("xq", idx) not in st:
+                st[("xq", idx)] = {}
+            for pi in which:
+                xg = st[("xg", idx)][pi]
                 xq = qpool.tile([P, NT], U32, name="xq", align_bytes=64)
                 xs = qpool.tile([P, NT], U8, name="xs", align_bytes=64)
                 nc.vector.quantize_mx(
                     out=xq[:].bitcast(FP8X4), scales=xs[:], in_=xg[:].rearrange("p w j -> p (w j)")
                 )
-                res.append((xq, xs))
-            st[("xq", idx)] = res
+                st[("xq", idx)][pi] = (xq, xs)
 
         def mm_half(idx, h):
             b, tl = idx // TILES, idx % TILES
@@ -366,8 +371,12 @@ def tile_attentionconv1d_t_kernel(tc, feature, embedding, weight, out):
                 math_3(1)
                 fix_f(1)
             if i == BPT - 1:
-                quantise(idx)
-                mm_half(idx, 0)
+                quantise(idx, (0, 1))
             if i == 0 and idx > 0:
+                quantise(idx - 1, (2,))
+                mm_half(idx - 1, 0)
+            if i == 1 and idx > 0:
                 mm_half(idx - 1, 1)
+        quantise(B * TILES - 1, (2,))
+        mm_half(B * TILES - 1, 0)
         mm_half(B * TILES - 1, 1)

from contextlib import ExitStack

import concourse.mybir as mybir
from concourse.masks import make_identity

B, C, T, O, KW = 2, 512, 3072, 512, 3
FLOPS = 2 * B * O * C * KW * T

P = 128
F32 = mybir.dt.float32
BF16 = mybir.dt.bfloat16
U32 = mybir.dt.uint32
U8 = mybir.dt.uint8
FP8X4 = mybir.dt.float8_e4m3fn_x4
MULT = mybir.AluOpType.mult
ADD = mybir.AluOpType.add
AXX = mybir.AxisListType.X

NT = 512
NBLK = T // P
TILES = T // NT
BPT = NT // P
EP = T + 16
FL = T + 32
FX = 2 * FL + 16
GN = 130
GB = 3
EPS2 = 1e-16

PASSES = (
    (2, 15, ((0, 0), (1, 0), (2, 1), (3, 1)), False),
    (2, 16, ((0, 1), (1, 1), (2, 2), (3, 2)), False),
    (0, 17, ((2, 0), (3, 0), (0, 2), (1, 2)), True),
)


def tile_attentionconv1d_t_kernel(tc, feature, embedding, weight, out):
    nc = tc.nc
    with ExitStack() as ctx:
        consts = ctx.enter_context(tc.tile_pool(name="consts", bufs=1))
        epool = ctx.enter_context(tc.tile_pool(name="epool", bufs=1))
        fpool = ctx.enter_context(tc.tile_pool(name="fpool", bufs=2))
        wts = ctx.enter_context(tc.tile_pool(name="wts", bufs=1))
        cols = ctx.enter_context(tc.tile_pool(name="cols", bufs=2))
        work = ctx.enter_context(tc.tile_pool(name="work", bufs=2))
        xpool = ctx.enter_context(tc.tile_pool(name="xpool", bufs=6))
        qpool = ctx.enter_context(tc.tile_pool(name="qpool", bufs=6))
        opool = ctx.enter_context(tc.tile_pool(name="opool", bufs=3))
        ypool = ctx.enter_context(tc.tile_pool(name="ypool", bufs=4))
        ps_g = ctx.enter_context(tc.psum_pool(name="ps_g", bufs=2))
        ps_x = ctx.enter_context(tc.psum_pool(name="ps_x", bufs=2))
        ps_y = ctx.enter_context(tc.psum_pool(name="ps_y", bufs=2))
        ps_o = ctx.enter_context(tc.psum_pool(name="ps_o", bufs=2))
        ctx.enter_context(tc.manual_schedule())

        def load_e(b):
            e_sb = epool.tile([P, 4, EP], BF16, name="e_sb")
            nc.gpsimd.memset(e_sb[:, :, T:EP], 0.0)
            half = T // 2
            for h in range(2):
                for j in range(4):
                    nc.sync.dma_start(
                        out=e_sb[:, j, h * half:(h + 1) * half],
                        in_=embedding[b, j * P:(j + 1) * P, h * half:(h + 1) * half],
                    )
            return e_sb

        def load_f(b):
            f_sb = fpool.tile([P, 6, FL], BF16, name="f_sb")
            nc.gpsimd.memset(f_sb[:, :, 0:32], 0.0)
            nc.gpsimd.memset(f_sb[:, :, T:FL], 0.0)
            return f_sb

        FH = 16 + T // 2

        def load_f_half(f_sb, b, h):
            for row, ch, shift in ((2, 0, 16), (3, 1, 16), (4, 2, 15), (5, 3, 15), (0, 2, 18), (1, 3, 18)):
                lo = max(shift, 16) if h == 0 else FH
                hi = FH if h == 0 else shift + T
                nc.sync.dma_start(
                    out=f_sb[:, row, lo:hi], in_=feature[b, ch * P:(ch + 1) * P, lo - shift:hi - shift]
                )

        def fix_f(b):
            f_sb = f_tiles[b]
            nc.vector.tensor_copy(out=f_sb[:, 4:6, 15:16], in_=f_sb[:, 0:2, 18:19])

        e_tiles = {}
        f_tiles = {}
        e_tiles[0] = load_e(0)
        f_tiles[0] = load_f(0)
        load_f_half(f_tiles[0], 0, 0)
        w_sb = wts.tile([P, 4, C * KW], BF16, name="w_sb")
        nc.sync.dma_start(out=w_sb[:], in_=weight.rearrange("(ot o) c k -> o ot (c k)", o=P))
        load_f_half(f_tiles[0], 0, 1)

        ident_f = consts.tile([P, P], F32, name="ident_f")
        make_identity(nc, ident_f[:])
        ident_b = consts.tile([P, P], BF16, name="ident_b")
        make_identity(nc, ident_b[:])
        warm = consts.tile([P, 1], F32, name="warm")
        nc.vector.memset(warm[:], 1.0)
        nc.scalar.sqrt(out=warm[:], in_=warm[:])
        band = consts.tile([P, GN], F32, name="band")
        nc.vector.memset(band[:], 0.0)
        nc.vector.tensor_copy(out=band[:, 0:P], in_=ident_f[:])
        nc.vector.tensor_add(out=band[:, 1:P + 1], in0=band[:, 1:P + 1], in1=ident_f[:])
        sh_up = consts.tile([P, P], F32, name="sh_up")
        e_up = consts.tile([P, P], F32, name="e_up")
        sh_dn = consts.tile([P, P], F32, name="sh_dn")
        e_dn = consts.tile([P, P], F32, name="e_dn")
        for t_ in (sh_up, e_up, sh_dn, e_dn):
            nc.vector.memset(t_[:], 0.0)
        nc.vector.tensor_copy(out=sh_up[:, 0:P - 1], in_=ident_f[:, 1:P])
        nc.vector.tensor_copy(out=e_up[:, P - 1:P], in_=ident_f[:, 0:1])
        nc.vector.tensor_copy(out=sh_dn[:, 1:P], in_=ident_f[:, 0:P - 1])
        nc.vector.tensor_copy(out=e_dn[:, 0:1], in_=ident_f[:, P - 1:P])
        par = consts.tile([P, 2], F32, name="par")
        nc.vector.tensor_reduce(
            out=par[:], in_=ident_f[:].rearrange("p (u v) -> p v u", v=2), axis=AXX, op=ADD
        )

        w_g = wts.tile([P, 3, 4 * NT], BF16, name="w_g", align_bytes=64)
        w_q = wts.tile([P, 3, NT], U32, name="w_q", align_bytes=64)
        w_s = wts.tile([P, 3, NT], U8, name="w_s", align_bytes=64)

        def weights_transpose(pi):
            slots = PASSES[pi][2]
            for ot in range(4):
                wt = ps_o.tile([P, 1024], BF16, name="wt", tag="o")
                for j in range(4):
                    ch, tau = slots[j]
                    src = w_sb[:, ot, :].rearrange("o (c k) -> o c k", k=KW)[:, ch * P:(ch + 1) * P, tau]
                    nc.tensor.transpose(wt[:, j * P:(j + 1) * P], src, ident_b[:])
                nc.scalar.copy(
                    out=w_g[:, pi, ot * NT:(ot + 1) * NT].rearrange("p (o j) -> p o j", j=4),
                    in_=wt[:, 0:NT].rearrange("p (j o) -> p o j", j=4),
                )

        def weights_quantise(pi):
            nc.vector.quantize_mx(
                out=w_q[:, pi, :].bitcast(FP8X4), scales=w_s[:, pi, :], in_=w_g[:, pi, :]
            )

        st = {}

        def gram_bank(b, k, pool, tag):
            e_sb = e_tiles[b]
            gp = pool.tile([P, 512], F32, name="gp", tag=tag)
            for i in range(GB):
                t0 = (k * GB + i) * P
                for j in range(4):
                    nc.tensor.matmul(
                        out=gp[:, i * GN:(i + 1) * GN],
                        lhsT=e_sb[:, j, t0:t0 + P],
                        rhs=e_sb[:, j, t0:t0 + GN],
                        start=(j == 0),
                        stop=(j == 3),
                    )
            st[("gp", b, k)] = gp

        def extract_bank(b, k):
            if k == 0:
                eo_new = cols.tile([P, NBLK, 2], F32, name="eo")
                st[("eo", b)] = eo_new
            eo = st[("eo", b)]
            gp = st[("gp", b, k)]
            gm = work.tile([P, GB, GN], F32, name="gm")
            nc.vector.tensor_tensor(
                out=gm[:],
                in0=gp[:, 0:GB * GN].rearrange("p (g n) -> p g n", g=GB),
                in1=band[:].unsqueeze(1).to_broadcast([P, GB, GN]),
                op=MULT,
            )
            nc.vector.tensor_reduce(
                out=eo[:, k * GB:(k + 1) * GB, :],
                in_=gm[:].rearrange("p g (u v) -> p g v u", v=2),
                axis=AXX,
                op=ADD,
            )

        CS = slice(1, NBLK + 1)

        def math_1(b):
            eo = st[("eo", b)]
            ev = eo[:, :, 0]
            od = eo[:, :, 1]
            t_a = cols.tile([P, NBLK], F32, name="t_a")
            t_b = cols.tile([P, NBLK], F32, name="t_b")
            n2 = cols.tile([P, NBLK], F32, name="n2")
            dd = cols.tile([P, NBLK], F32, name="dd")
            nc.vector.tensor_scalar_mul(out=t_a[:], in0=ev, scalar1=par[:, 0:1])
            nc.vector.tensor_scalar_mul(out=t_b[:], in0=ev, scalar1=par[:, 1:2])
            nc.vector.scalar_tensor_tensor(out=n2[:], in0=od, scalar=par[:, 1:2], in1=t_a[:], op0=MULT, op1=ADD)
            nc.vector.scalar_tensor_tensor(out=dd[:], in0=od, scalar=par[:, 0:1], in1=t_b[:], op0=MULT, op1=ADD)
            m2 = cols.tile([P, NBLK], F32, name="m2")
            nc.vector.tensor_scalar_max(out=m2[:], in0=n2[:], scalar1=EPS2)
            sq = cols.tile([P, NBLK], F32, name="sq")
            nc.scalar.sqrt(out=sq[:], in_=m2[:])
            rn = cols.tile([P, NBLK + 2], F32, name="rn")
            nc.vector.memset(rn[:], 0.0)
            aa = cols.tile([P, NBLK + 2], F32, name="aa")
            nc.vector.memset(aa[:], 0.0)
            st[("m1", b)] = (n2, dd, m2, sq, rn, aa)

        def math_2(b):
            n2, dd, m2, sq, rn, aa = st[("m1", b)]
            y0 = cols.tile([P, NBLK], F32, name="y0")
            nc.vector.reciprocal(out=y0[:], in_=sq[:])
            u1 = cols.tile([P, NBLK], F32, name="u1")
            nc.vector.tensor_mul(out=u1[:], in0=y0[:], in1=y0[:])
            u2 = cols.tile([P, NBLK], F32, name="u2")
            nc.vector.tensor_mul(out=u2[:], in0=u1[:], in1=m2[:])
            u3 = cols.tile([P, NBLK], F32, name="u3")
            nc.vector.tensor_scalar(out=u3[:], in0=u2[:], scalar1=-0.5, scalar2=1.5, op0=MULT, op1=ADD)
            nc.vector.tensor_mul(out=rn[:, CS], in0=y0[:], in1=u3[:])
            nc.vector.tensor_mul(out=aa[:, CS], in0=dd[:], in1=rn[:, CS])
            sh = ps_g.tile([P, 512], F32, name="sh", tag="g")
            nc.tensor.matmul(out=sh[:, 0:NBLK], lhsT=sh_up[:], rhs=rn[:, 1:NBLK + 1], start=True, stop=False)
            nc.tensor.matmul(out=sh[:, 0:NBLK], lhsT=e_up[:], rhs=rn[:, 2:NBLK + 2], start=False, stop=True)
            nc.tensor.matmul(out=sh[:, 64:64 + NBLK], lhsT=sh_dn[:], rhs=aa[:, 1:NBLK + 1], start=True, stop=False)
            nc.tensor.matmul(out=sh[:, 64:64 + NBLK], lhsT=e_dn[:], rhs=aa[:, 0:NBLK], start=False, stop=True)
            r2 = cols.tile([P, NBLK], F32, name="r2")
            nc.vector.tensor_mul(out=r2[:], in0=rn[:, CS], in1=rn[:, CS])
            sim_c = cols.tile([P, NBLK], F32, name="sim_c")
            nc.vector.tensor_mul(out=sim_c[:], in0=n2[:], in1=r2[:])
            st[("m2", b)] = (sh, sim_c)

        def math_3(b):
            n2, dd, m2, sq, rn, aa = st[("m1", b)]
            sh, sim_c = st[("m2", b)]
            sim_r = cols.tile([P, NBLK], F32, name="sim_r")
            nc.vector.tensor_mul(out=sim_r[:], in0=aa[:, CS], in1=sh[:, 0:NBLK])
            sim_l = cols.tile([P, NBLK], F32, name="sim_l")
            nc.vector.tensor_mul(out=sim_l[:], in0=rn[:, CS], in1=sh[:, 64:64 + NBLK])
            st[("sim", b)] = (sim_l, sim_c, sim_r)

        def build_w(idx):
            b, tl = idx // TILES, idx % TILES
            sim_l, sim_c, sim_r = st[("sim", b)]
            c0 = tl * BPT
            w1 = work.tile([P, BPT, 132], F32, name="w1")
            w2 = work.tile([P, BPT, 132], F32, name="w2")

            def spread(dst, src, n):
                nc.scalar.copy(out=dst, in_=src[:, c0:c0 + BPT].unsqueeze(2).to_broadcast([P, BPT, n]))

            spread(w1[:, :, 0:43], sim_l, 43)
            spread(w1[:, :, 43:129], sim_c, 86)
            spread(w2[:, :, 0:86], sim_c, 86)
            spread(w2[:, :, 86:129], sim_r, 43)
            st[("w", idx)] = (w1, w2)

        def tr_block(g):
            idx, i = g // BPT, g % BPT
            b, tl = idx // TILES, idx % TILES
            sim_l, sim_c, sim_r = st[("sim", b)]
            w1, w2 = st[("w", idx)]
            c = tl * BPT + i
            left = sim_l[:, c:c + 1].to_broadcast([P, P])
            right = sim_r[:, c:c + 1].to_broadcast([P, P])
            xb = ps_x.tile([P, 512], F32, name="xb", tag="xb")
            yb = ps_y.tile([P, 512], F32, name="yb", tag="yb")
            for j, src in enumerate((left, w1[:, i, 0:P], w2[:, i, 1:P + 1], right)):
                nc.tensor.transpose(xb[:, j * P:(j + 1) * P], src, ident_f[:])
            for j, src in enumerate((w2[:, i, 0:P], right, left, w1[:, i, 1:P + 1])):
                nc.tensor.transpose(yb[:, j * P:(j + 1) * P], src, ident_f[:])
            y_sb = ypool.tile([P, 512], F32, name="y_sb")
            nc.scalar.copy(out=y_sb[:], in_=yb[:])
            st[("s", g)] = (xb, y_sb)

        def mult_block(g):
            idx, i = g // BPT, g % BPT
            b, tl = idx // TILES, idx % TILES
            f_sb = f_tiles[b]
            if i == 0:
                xg_new = []
                for pi in range(3):
                    xg = xpool.tile([P, NT, 4], BF16, name="xg", align_bytes=64)
                    xg_new.append(xg)
                st[("xg", idx)] = xg_new
            xgs = st[("xg", idx)]
            xb, yb = st[("s", g)]
            for pi, (r0, col0, slots, second) in enumerate(PASSES):
                s0 = col0 + tl * NT + i * P
                bank = yb if second else xb
                eng = nc.gpsimd if second else nc.vector
                eng.tensor_tensor(
                    out=xgs[pi][:, i * P:(i + 1) * P, :].rearrange("p (c i) j -> p c j i", i=4),
                    in0=f_sb[:, r0:r0 + 4, s0:s0 + P].rearrange("p j (c i) -> p c j i", i=4),
                    in1=bank[:].rearrange("p (j c i) -> p c j i", j=4, i=4),
                    op=MULT,
                )

        def quantise(idx, which):
            if ("xq", idx) not in st:
                st[("xq", idx)] = {}
            for pi in which:
                xg = st[("xg", idx)][pi]
                xq = qpool.tile([P, NT], U32, name="xq", align_bytes=64)
                xs = qpool.tile([P, NT], U8, name="xs", align_bytes=64)
                nc.vector.quantize_mx(
                    out=xq[:].bitcast(FP8X4), scales=xs[:], in_=xg[:].rearrange("p w j -> p (w j)")
                )
                st[("xq", idx)][pi] = (xq, xs)

        def mm_half(idx, h):
            b, tl = idx // TILES, idx % TILES
            t0 = tl * NT
            xqs = st[("xq", idx)]
            o_sb = opool.tile([P, 2, NT], F32, name="o_sb")
            for oo in range(2):
                ot = 2 * h + oo
                acc = ps_o.tile([P, NT], F32, name="acc", tag="o")
                for pi in range(3):
                    xq, xs = xqs[pi]
                    nc.tensor.matmul_mx(
                        out=acc[:],
                        lhsT=w_q[:, pi, ot * P:(ot + 1) * P].bitcast(FP8X4),
                        lhsT_scale=w_s[:, pi, ot * P:(ot + 1) * P],
                        rhs=xq[:].bitcast(FP8X4),
                        rhs_scale=xs[:],
                        start=(pi == 0),
                        stop=(pi == 2),
                    )
                nc.scalar.copy(out=o_sb[:, oo, :], in_=acc[:])
            nc.sync.dma_start(
                out=out[b, 2 * h * P:(2 * h + 2) * P, t0:t0 + NT].rearrange("(ot p) t -> p ot t", p=P),
                in_=o_sb[:],
            )

        rot = ((ps_g, "g"), (ps_g, "g"), (ps_x, "xb"), (ps_x, "xb"), (ps_y, "yb"), (ps_y, "yb"), (ps_o, "o"), (ps_o, "o"))
        NBANK = NBLK // GB
        for k in range(NBANK):
            gram_bank(0, k, rot[k][0], rot[k][1])
        for k in range(NBANK):
            extract_bank(0, k)
        math_1(0)
        math_2(0)
        math_3(0)
        e_tiles[1] = load_e(1)
        f_tiles[1] = load_f(1)
        load_f_half(f_tiles[1], 1, 0)
        load_f_half(f_tiles[1], 1, 1)
        fix_f(0)
        build_w(0)
        tr_block(0)
        tr_block(1)

        NG = B * NBLK
        for g in range(NG):
            idx, i = g // BPT, g % BPT
            if i == 0 and idx + 1 < B * TILES:
                build_w(idx + 1)
            mult_block(g)
            if g + 2 < NG:
                tr_block(g + 2)
            if g < 3:
                weights_transpose(g)
            if 1 <= g < 4:
                weights_quantise(g - 1)
            if 4 <= g < 4 + NBANK:
                gram_bank(1, g - 4, ps_g, "g")
            if 5 <= g < 5 + NBANK:
                extract_bank(1, g - 5)
            if g == 13:
                math_1(1)
            if g == 14:
                math_2(1)
            if g == 15:
                math_3(1)
                fix_f(1)
            if i == BPT - 1:
                quantise(idx, (0, 1))
            if i == 0 and idx > 0:
                quantise(idx - 1, (2,))
                mm_half(idx - 1, 0)
            if i == 1 and idx > 0:
                mm_half(idx - 1, 1)
        quantise(B * TILES - 1, (2,))
        mm_half(B * TILES - 1, 0)
        mm_half(B * TILES - 1, 1)
